import numpy as np
import ml_dtypes


def mxq(x, axis, fmt="e4m3"):
    dtype, down = {"e4m3": (ml_dtypes.float8_e4m3fn, 7), "e5m2": (ml_dtypes.float8_e5m2, 14)}[fmt]
    v = np.moveaxis(np.asarray(x, np.float32).astype(ml_dtypes.bfloat16).astype(np.float64), axis, -1)
    blocks = v.reshape(v.shape[:-1] + (-1, 32))
    amax = np.abs(blocks).max(-1, keepdims=True)
    byte = np.maximum(np.where(amax > 0, np.frexp(amax)[1] - 1 + 127, 0) - down, 1)
    scale = np.exp2(byte - 127.0)
    codes = (blocks / scale).astype(np.float32).astype(dtype).astype(np.float64)
    return np.moveaxis((codes * scale).reshape(v.shape), -1, axis)


WIDE = False


def mx_kscale(k):
    if not WIDE:
        return np.ones(k)
    levels = np.array([10, -10, 5, -5, 0])
    a = np.random.permutation(np.resize(levels, k // 512 * 4)).reshape(k // 512, 4)
    idx = np.arange(k)
    return np.exp2(a[idx // 512, idx % 128 // 32])


BF16 = ml_dtypes.bfloat16


def bf(x):
    return np.asarray(x, np.float32).astype(BF16)


def f64(x):
    return np.asarray(x).astype(np.float64)


B, S, C, O, G = 4, 2048, 512, 512, 128
NG = C // G
SCALE_MIN = 1e-8


def quantize_literati(weight, scales):
    wg = weight.reshape(O, NG, G)
    signs = np.where(wg >= 0, 1.0, -1.0)
    s = np.maximum(scales, SCALE_MIN)
    w_q = signs * s[..., None]
    return w_q.reshape(O, C)


def setup_inputs():
    sr = mx_kscale(C).reshape(NG, G)
    g = np.where(np.arange(NG) % 2 == 0, sr.max(1), sr.min(1))
    bound = 1.0 / np.sqrt(C)
    return {"x": bf(np.random.standard_normal((B, S, C)) * np.repeat(g, G)),
            "weight": bf(np.random.uniform(-bound, bound, (O, C))),
            "scales": bf((1.0 + 0.5 * np.random.standard_normal((O, NG))) / np.sqrt(C) / g)}


def reference(x, weight, scales):
    w_q = quantize_literati(f64(weight), f64(scales))
    return mxq(f64(x), 2, "e4m3") @ mxq(w_q, 1, "e4m3").T

@@ -1,0 +1,190 @@
+from contextlib import ExitStack
+
+import concourse.mybir as mybir
+from concourse.masks import make_identity
+
+FP8X4 = mybir.dt.float8_e4m3fn_x4
+BF16 = mybir.dt.bfloat16
+F32 = mybir.dt.float32
+U32 = mybir.dt.uint32
+U8 = mybir.dt.uint8
+ALU = mybir.AluOpType
+
+P = 128
+ROWS = 4 * 2048
+C = 512
+O = 512
+ROW_TILES = ROWS // P
+GROUP = 4
+GROUPS = ROW_TILES // GROUP
+STORE = 8
+SCALE_MIN = 1e-8
+
+FLOPS = 2 * ROWS * C * O
+
+LOADS = [(0, 4), (4, 8)] + [(j, j + 8) for j in range(8, ROW_TILES, 8)]
+
+
+def tile_literatiquantlinear_t_kernel(tc, x, weight, scales, out):
+    nc = tc.nc
+    x_rows = x.rearrange("b (q j) c -> (b q) j c", j=ROW_TILES)
+    out_rows = out.rearrange("b (q j) o -> (b q) j o", j=ROW_TILES)
+
+    with ExitStack() as ctx:
+        const = ctx.enter_context(tc.tile_pool(name="const", bufs=1))
+        xpool = ctx.enter_context(tc.tile_pool(name="xpool", bufs=1))
+        gpool = ctx.enter_context(tc.tile_pool(name="gpool", bufs=3))
+        cpool = ctx.enter_context(tc.tile_pool(name="cpool", bufs=3))
+        opool = ctx.enter_context(tc.tile_pool(name="opool", bufs=6))
+        tpsum = ctx.enter_context(tc.psum_pool(name="tpsum", bufs=4))
+        apsum = ctx.enter_context(tc.psum_pool(name="apsum", bufs=4))
+        ctx.enter_context(tc.manual_schedule())
+
+        s_sb = const.tile([P, 4, 4], BF16, name="s_sb")
+        nc.sync.dma_start(out=s_sb[:], in_=scales.rearrange("(t p) g -> p t g", p=P))
+        w_sb = const.tile([P, 4, C], BF16, name="w_sb")
+        nc.sync.dma_start(out=w_sb[:], in_=weight.rearrange("(t p) c -> p t c", p=P))
+        x_tiles = []
+        where = {}
+        for li, (j0, j1) in enumerate(LOADS):
+            xt_sb = xpool.tile([P, (j1 - j0) * C], BF16, name="x%d" % li)
+            nc.sync.dma_start(
+                out=xt_sb[:].rearrange("p (j c) -> p j c", c=C), in_=x_rows[:, j0:j1, :]
+            )
+            x_tiles.append(xt_sb)
+            for j in range(j0, j1):
+                where[j] = (li, j - j0)
+
+        ident_f = const.tile([P, P], F32, name="ident_f")
+        make_identity(nc, ident_f[:])
+        ident_b = const.tile([P, P], BF16, name="ident_b")
+        make_identity(nc, ident_b[:])
+
+        def x_words(j):
+            li, off = where[j]
+            words = x_tiles[li][:, off * C : (off + 1) * C].bitcast(F32)
+            return words.rearrange("p (w u) -> p u w", u=2)
+
+        grouped = {}
+        codes = {}
+        planes = {}
+
+        def transposes(g, copy_engine):
+            gr = gpool.tile([P, GROUP * C], BF16, name="gr", align_bytes=64)
+            grouped[g] = gr
+            gr_words = gr[:].bitcast(F32)
+            for h in range(GROUP // 2):
+                xt = tpsum.tile([P, 2, 2, P], F32, name="xt", tag="xt")
+                for jj in range(2):
+                    src = x_words(GROUP * g + 2 * h + jj)
+                    for u in range(2):
+                        nc.tensor.transpose(
+                            out=xt[:, jj, u, :], in_=src[:, u, :], identity=ident_f[:]
+                        )
+                dst = gr_words[:, h * C : (h + 1) * C].rearrange(
+                    "p (j r u) -> p j r u", j=2, u=2
+                )
+                view = xt[:].rearrange("p j u r -> p j r u")
+                if copy_engine == "scalar":
+                    nc.scalar.copy(out=dst, in_=view)
+                else:
+                    nc.vector.tensor_copy(out=dst, in_=view)
+
+        def quantise(g):
+            cd = cpool.tile([P, GROUP * P], U32, name="cd", align_bytes=64)
+            pl = cpool.tile([P, GROUP * P], U8, name="pl", align_bytes=64)
+            codes[g] = cd
+            planes[g] = pl
+            nc.vector.quantize_mx(out=cd[:].bitcast(FP8X4), scales=pl[:], in_=grouped[g][:])
+
+        out_tiles = {}
+
+        def multiply(g):
+            chunk = (GROUP * g) // STORE
+            if chunk not in out_tiles:
+                o_new = opool.tile([P, STORE, O], F32, name="o_sb", tag="o_sb")
+                out_tiles[chunk] = o_new
+            o_sb = out_tiles[chunk]
+            for jj in range(GROUP):
+                j = GROUP * g + jj
+                acc = apsum.tile([P, O], F32, name="acc", tag="acc")
+                nc.tensor.matmul_mx(
+                    out=acc[:],
+                    lhsT=codes[g][:, jj * P : (jj + 1) * P].bitcast(FP8X4),
+                    lhsT_scale=planes[g][:, jj * P : (jj + 1) * P],
+                    rhs=w_codes[:].bitcast(FP8X4),
+                    rhs_scale=w_plane[:],
+                    start=True,
+                    stop=True,
+                )
+                if g % 2 == 1 and jj == 0:
+                    nc.vector.tensor_copy(out=o_sb[:, j % STORE, :], in_=acc[:])
+                else:
+                    nc.scalar.copy(out=o_sb[:, j % STORE, :], in_=acc[:])
+            last = chunk == ROW_TILES // STORE - 1
+            j_end = GROUP * (g + 1)
+            if last:
+                j_start = GROUP * g
+                nc.sync.dma_start(
+                    out=out_rows[:, j_start:j_end, :],
+                    in_=o_sb[:, j_start % STORE : j_start % STORE + GROUP, :],
+                )
+            elif j_end % STORE == 0:
+                nc.sync.dma_start(out=out_rows[:, j_end - STORE : j_end, :], in_=o_sb[:])
+
+        s2 = const.tile([P, 16], F32, name="s2")
+        nc.vector.tensor_scalar(
+            out=s2[:],
+            in0=s_sb[:].rearrange("p t g -> p (t g)"),
+            scalar1=SCALE_MIN,
+            scalar2=2.0,
+            op0=ALU.max,
+            op1=ALU.mult,
+        )
+        half = const.tile([P, 4, C], BF16, name="half")
+        wq = const.tile([P, 4, 4, P], BF16, name="wq")
+        for ot in range(4):
+            nc.vector.tensor_scalar(
+                out=half[:, ot, :],
+                in0=w_sb[:, ot, :],
+                scalar1=0.0,
+                scalar2=0.5,
+                op0=ALU.is_ge,
+                op1=ALU.subtract,
+            )
+            nc.vector.tensor_tensor(
+                out=wq[:, ot, :, :].rearrange("o t (g q) -> o t g q", g=4),
+                in0=half[:, ot, :].rearrange("o (g q t) -> o t g q", g=4, t=4),
+                in1=s2[:, 4 * ot : 4 * ot + 4]
+                .unsqueeze(1)
+                .unsqueeze(3)
+                .to_broadcast([P, 4, 4, 32]),
+                op=ALU.mult,
+            )
+
+        transposes(0, "scalar")
+
+        wg = const.tile([P, O, 4], BF16, name="wg", align_bytes=64)
+        for ot in range(4):
+            wt = tpsum.tile([P, 4, P], BF16, name="wt", tag="xt")
+            for t in range(4):
+                nc.tensor.transpose(out=wt[:, t, :], in_=wq[:, ot, t, :], identity=ident_b[:])
+            nc.scalar.copy(
+                out=wg[:, ot * P : (ot + 1) * P, :], in_=wt[:].rearrange("p t o -> p o t")
+            )
+        w_codes = const.tile([P, O], U32, name="w_codes", align_bytes=64)
+        w_plane = const.tile([P, O], U8, name="w_plane", align_bytes=64)
+        nc.vector.quantize_mx(
+            out=w_codes[:].bitcast(FP8X4),
+            scales=w_plane[:],
+            in_=wg[:].rearrange("p o t -> p (o t)"),
+        )
+        quantise(0)
+
+        for i in range(1, GROUPS + 2):
+            if i < GROUPS:
+                transposes(i, "vector")
+            if 2 <= i <= GROUPS:
+                quantise(i - 1)
+            if i >= 2:
+                multiply(i - 2)

@@ -63,7 +63,7 @@ def tile_literatiquantlinear_t_kernel(tc, x, weight, scales, out):
         def x_words(j):
             li, off = where[j]
             words = x_tiles[li][:, off * C : (off + 1) * C].bitcast(F32)
-            return words.rearrange("p (w u) -> p u w", u=2)
+            return words.rearrange("p (u w) -> p u w", u=2)
 
         grouped = {}
         codes = {}
@@ -152,15 +152,18 @@ def tile_literatiquantlinear_t_kernel(tc, x, weight, scales, out):
                 op0=ALU.is_ge,
                 op1=ALU.subtract,
             )
-            nc.vector.tensor_tensor(
-                out=wq[:, ot, :, :].rearrange("o t (g q) -> o t g q", g=4),
-                in0=half[:, ot, :].rearrange("o (g q t) -> o t g q", g=4, t=4),
-                in1=s2[:, 4 * ot : 4 * ot + 4]
-                .unsqueeze(1)
-                .unsqueeze(3)
-                .to_broadcast([P, 4, 4, 32]),
-                op=ALU.mult,
-            )
+            for u in range(2):
+                nc.vector.tensor_tensor(
+                    out=wq[:, ot, 2 * u : 2 * u + 2, :].rearrange("o e (h q) -> o e h q", h=2),
+                    in0=half[:, ot, 256 * u : 256 * u + 256].rearrange(
+                        "o (h q e) -> o e h q", h=2, e=2
+                    ),
+                    in1=s2[:, 4 * ot + 2 * u : 4 * ot + 2 * u + 2]
+                    .unsqueeze(1)
+                    .unsqueeze(3)
+                    .to_broadcast([P, 2, 2, 64]),
+                    op=ALU.mult,
+                )
 
         transposes(0, "scalar")
 

@@ -22,7 +22,7 @@ SCALE_MIN = 1e-8
 
 FLOPS = 2 * ROWS * C * O
 
-LOADS = [(0, 4), (4, 8)] + [(j, j + 8) for j in range(8, ROW_TILES, 8)]
+LOADS = [(0, 4), (4, 8), (8, 16), (16, 32), (32, 48), (48, 64)]
 
 
 def tile_literatiquantlinear_t_kernel(tc, x, weight, scales, out):
@@ -40,10 +40,10 @@ def tile_literatiquantlinear_t_kernel(tc, x, weight, scales, out):
         apsum = ctx.enter_context(tc.psum_pool(name="apsum", bufs=4))
         ctx.enter_context(tc.manual_schedule())
 
-        s_sb = const.tile([P, 4, 4], BF16, name="s_sb")
-        nc.sync.dma_start(out=s_sb[:], in_=scales.rearrange("(t p) g -> p t g", p=P))
+        s_sb = const.tile([P, 16], BF16, name="s_sb")
+        nc.sync.dma_start(out=s_sb[:], in_=scales.rearrange("(p t) g -> p (t g)", t=4))
         w_sb = const.tile([P, 4, C], BF16, name="w_sb")
-        nc.sync.dma_start(out=w_sb[:], in_=weight.rearrange("(t p) c -> p t c", p=P))
+        nc.sync.dma_start(out=w_sb[:], in_=weight.rearrange("(p t) c -> p t c", t=4))
         x_tiles = []
         where = {}
         for li, (j0, j1) in enumerate(LOADS):
@@ -63,7 +63,7 @@ def tile_literatiquantlinear_t_kernel(tc, x, weight, scales, out):
         def x_words(j):
             li, off = where[j]
             words = x_tiles[li][:, off * C : (off + 1) * C].bitcast(F32)
-            return words.rearrange("p (u w) -> p u w", u=2)
+            return words.rearrange("p (w u) -> p u w", u=2)
 
         grouped = {}
         codes = {}
@@ -135,7 +135,7 @@ def tile_literatiquantlinear_t_kernel(tc, x, weight, scales, out):
         s2 = const.tile([P, 16], F32, name="s2")
         nc.vector.tensor_scalar(
             out=s2[:],
-            in0=s_sb[:].rearrange("p t g -> p (t g)"),
+            in0=s_sb[:],
             scalar1=SCALE_MIN,
             scalar2=2.0,
             op0=ALU.max,
@@ -152,18 +152,15 @@ def tile_literatiquantlinear_t_kernel(tc, x, weight, scales, out):
                 op0=ALU.is_ge,
                 op1=ALU.subtract,
             )
-            for u in range(2):
-                nc.vector.tensor_tensor(
-                    out=wq[:, ot, 2 * u : 2 * u + 2, :].rearrange("o e (h q) -> o e h q", h=2),
-                    in0=half[:, ot, 256 * u : 256 * u + 256].rearrange(
-                        "o (h q e) -> o e h q", h=2, e=2
-                    ),
-                    in1=s2[:, 4 * ot + 2 * u : 4 * ot + 2 * u + 2]
-                    .unsqueeze(1)
-                    .unsqueeze(3)
-                    .to_broadcast([P, 2, 2, 64]),
-                    op=ALU.mult,
-                )
+            nc.vector.tensor_tensor(
+                out=wq[:, ot, :, :].rearrange("o t (g q) -> o t g q", g=4),
+                in0=half[:, ot, :].rearrange("o (g q t) -> o t g q", g=4, t=4),
+                in1=s2[:, 4 * ot : 4 * ot + 4]
+                .unsqueeze(1)
+                .unsqueeze(3)
+                .to_broadcast([P, 4, 4, 32]),
+                op=ALU.mult,
+            )
 
         transposes(0, "scalar")
 
@@ -173,7 +170,8 @@ def tile_literatiquantlinear_t_kernel(tc, x, weight, scales, out):
             for t in range(4):
                 nc.tensor.transpose(out=wt[:, t, :], in_=wq[:, ot, t, :], identity=ident_b[:])
             nc.scalar.copy(
-                out=wg[:, ot * P : (ot + 1) * P, :], in_=wt[:].rearrange("p t o -> p o t")
+                out=wg[:].rearrange("p (col tp) t -> p col tp t", tp=4)[:, :, ot, :],
+                in_=wt[:].rearrange("p t col -> p col t"),
             )
         w_codes = const.tile([P, O], U32, name="w_codes", align_bytes=64)
         w_plane = const.tile([P, O], U8, name="w_plane", align_bytes=64)

@@ -57,8 +57,6 @@ def tile_literatiquantlinear_t_kernel(tc, x, weight, scales, out):
 
         ident_f = const.tile([P, P], F32, name="ident_f")
         make_identity(nc, ident_f[:])
-        ident_b = const.tile([P, P], BF16, name="ident_b")
-        make_identity(nc, ident_b[:])
 
         def x_words(j):
             li, off = where[j]
@@ -69,26 +67,28 @@ def tile_literatiquantlinear_t_kernel(tc, x, weight, scales, out):
         codes = {}
         planes = {}
 
-        def transposes(g, copy_engine):
-            gr = gpool.tile([P, GROUP * C], BF16, name="gr", align_bytes=64)
-            grouped[g] = gr
-            gr_words = gr[:].bitcast(F32)
+        def transpose_half(g, h, copy_engine):
+            if g not in grouped:
+                gr_new = gpool.tile([P, GROUP * C], BF16, name="gr", align_bytes=64)
+                grouped[g] = gr_new
+            gr_words = grouped[g][:].bitcast(F32)
+            xt = tpsum.tile([P, 2, 2, P], F32, name="xt", tag="xt")
+            for jj in range(2):
+                src = x_words(GROUP * g + 2 * h + jj)
+                for u in range(2):
+                    nc.tensor.transpose(
+                        out=xt[:, jj, u, :], in_=src[:, u, :], identity=ident_f[:]
+                    )
+            dst = gr_words[:, h * C : (h + 1) * C].rearrange("p (j r u) -> p j r u", j=2, u=2)
+            view = xt[:].rearrange("p j u r -> p j r u")
+            if copy_engine == "scalar":
+                nc.scalar.copy(out=dst, in_=view)
+            else:
+                nc.vector.tensor_copy(out=dst, in_=view)
+
+        def transposes(g):
             for h in range(GROUP // 2):
-                xt = tpsum.tile([P, 2, 2, P], F32, name="xt", tag="xt")
-                for jj in range(2):
-                    src = x_words(GROUP * g + 2 * h + jj)
-                    for u in range(2):
-                        nc.tensor.transpose(
-                            out=xt[:, jj, u, :], in_=src[:, u, :], identity=ident_f[:]
-                        )
-                dst = gr_words[:, h * C : (h + 1) * C].rearrange(
-                    "p (j r u) -> p j r u", j=2, u=2
-                )
-                view = xt[:].rearrange("p j u r -> p j r u")
-                if copy_engine == "scalar":
-                    nc.scalar.copy(out=dst, in_=view)
-                else:
-                    nc.vector.tensor_copy(out=dst, in_=view)
+                transpose_half(g, h, "vector")
 
         def quantise(g):
             cd = cpool.tile([P, GROUP * P], U32, name="cd", align_bytes=64)
@@ -142,49 +142,61 @@ def tile_literatiquantlinear_t_kernel(tc, x, weight, scales, out):
             op1=ALU.mult,
         )
         half = const.tile([P, 4, C], BF16, name="half")
-        wq = const.tile([P, 4, 4, P], BF16, name="wq")
-        for ot in range(4):
+        wq = const.tile([P, 4, C], BF16, name="wq")
+        wg = const.tile([P, O * 4], BF16, name="wg", align_bytes=64)
+        wg_words = wg[:].bitcast(F32).rearrange("p (r ot u) -> p r ot u", ot=4, u=2)
+
+        def signs_times_scales(h):
             nc.vector.tensor_scalar(
-                out=half[:, ot, :],
-                in0=w_sb[:, ot, :],
+                out=half[:, 2 * h : 2 * h + 2, :],
+                in0=w_sb[:, 2 * h : 2 * h + 2, :],
                 scalar1=0.0,
                 scalar2=0.5,
                 op0=ALU.is_ge,
                 op1=ALU.subtract,
             )
-            nc.vector.tensor_tensor(
-                out=wq[:, ot, :, :].rearrange("o t (g q) -> o t g q", g=4),
-                in0=half[:, ot, :].rearrange("o (g q t) -> o t g q", g=4, t=4),
-                in1=s2[:, 4 * ot : 4 * ot + 4]
-                .unsqueeze(1)
-                .unsqueeze(3)
-                .to_broadcast([P, 4, 4, 32]),
-                op=ALU.mult,
-            )
+            for ot in (2 * h, 2 * h + 1):
+                for g in range(4):
+                    cols = slice(g * P, (g + 1) * P)
+                    nc.vector.tensor_scalar(
+                        out=wq[:, ot, cols],
+                        in0=half[:, ot, cols],
+                        scalar1=s2[:, 4 * ot + g : 4 * ot + g + 1],
+                        scalar2=None,
+                        op0=ALU.mult,
+                    )
 
-        transposes(0, "scalar")
-
-        wg = const.tile([P, O, 4], BF16, name="wg", align_bytes=64)
-        for ot in range(4):
-            wt = tpsum.tile([P, 4, P], BF16, name="wt", tag="xt")
-            for t in range(4):
-                nc.tensor.transpose(out=wt[:, t, :], in_=wq[:, ot, t, :], identity=ident_b[:])
+        def weight_transposes(h):
+            wt = tpsum.tile([P, 2, 2, P], F32, name="wt", tag="xt")
+            for oo in range(2):
+                words = wq[:, 2 * h + oo, :].bitcast(F32).rearrange("p (w u) -> p u w", u=2)
+                for u in range(2):
+                    nc.tensor.transpose(
+                        out=wt[:, oo, u, :], in_=words[:, u, :], identity=ident_f[:]
+                    )
             nc.scalar.copy(
-                out=wg[:].rearrange("p (col tp) t -> p col tp t", tp=4)[:, :, ot, :],
-                in_=wt[:].rearrange("p t col -> p col t"),
+                out=wg_words[:, :, 2 * h : 2 * h + 2, :],
+                in_=wt[:].rearrange("p ot u r -> p r ot u"),
             )
+
+        signs_times_scales(0)
+        signs_times_scales(1)
+        weight_transposes(0)
+        transpose_half(0, 0, "vector")
+        weight_transposes(1)
+        transpose_half(0, 1, "scalar")
         w_codes = const.tile([P, O], U32, name="w_codes", align_bytes=64)
         w_plane = const.tile([P, O], U8, name="w_plane", align_bytes=64)
         nc.vector.quantize_mx(
             out=w_codes[:].bitcast(FP8X4),
             scales=w_plane[:],
-            in_=wg[:].rearrange("p o t -> p (o t)"),
+            in_=wg[:],
         )
         quantise(0)
 
         for i in range(1, GROUPS + 2):
             if i < GROUPS:
-                transposes(i, "vector")
+                transposes(i)
             if 2 <= i <= GROUPS:
                 quantise(i - 1)
             if i >= 2:

@@ -17,7 +17,7 @@ O = 512
 ROW_TILES = ROWS // P
 GROUP = 4
 GROUPS = ROW_TILES // GROUP
-STORE = 8
+STORE = 4
 SCALE_MIN = 1e-8
 
 FLOPS = 2 * ROWS * C * O
@@ -35,7 +35,7 @@ def tile_literatiquantlinear_t_kernel(tc, x, weight, scales, out):
         xpool = ctx.enter_context(tc.tile_pool(name="xpool", bufs=1))
         gpool = ctx.enter_context(tc.tile_pool(name="gpool", bufs=3))
         cpool = ctx.enter_context(tc.tile_pool(name="cpool", bufs=3))
-        opool = ctx.enter_context(tc.tile_pool(name="opool", bufs=6))
+        opool = ctx.enter_context(tc.tile_pool(name="opool", bufs=12))
         tpsum = ctx.enter_context(tc.psum_pool(name="tpsum", bufs=4))
         apsum = ctx.enter_context(tc.psum_pool(name="apsum", bufs=4))
         ctx.enter_context(tc.manual_schedule())

@@ -48,7 +48,7 @@ def tile_literatiquantlinear_t_kernel(tc, x, weight, scales, out):
         where = {}
         for li, (j0, j1) in enumerate(LOADS):
             xt_sb = xpool.tile([P, (j1 - j0) * C], BF16, name="x%d" % li)
-            nc.sync.dma_start(
+            nc.scalar.dma_start(
                 out=xt_sb[:].rearrange("p (j c) -> p j c", c=C), in_=x_rows[:, j0:j1, :]
             )
             x_tiles.append(xt_sb)

@@ -17,6 +17,7 @@ O = 512
 ROW_TILES = ROWS // P
 GROUP = 4
 GROUPS = ROW_TILES // GROUP
+DMA_ALIGN = 512
 STORE = 4
 SCALE_MIN = 1e-8
 
@@ -40,14 +41,16 @@ def tile_literatiquantlinear_t_kernel(tc, x, weight, scales, out):
         apsum = ctx.enter_context(tc.psum_pool(name="apsum", bufs=4))
         ctx.enter_context(tc.manual_schedule())
 
-        s_sb = const.tile([P, 16], BF16, name="s_sb")
+        s_sb = const.tile([P, 16], BF16, name="s_sb", align_bytes=DMA_ALIGN)
         nc.sync.dma_start(out=s_sb[:], in_=scales.rearrange("(p t) g -> p (t g)", t=4))
-        w_sb = const.tile([P, 4, C], BF16, name="w_sb")
+        w_sb = const.tile([P, 4, C], BF16, name="w_sb", align_bytes=DMA_ALIGN)
         nc.sync.dma_start(out=w_sb[:], in_=weight.rearrange("(p t) c -> p t c", t=4))
         x_tiles = []
         where = {}
         for li, (j0, j1) in enumerate(LOADS):
-            xt_sb = xpool.tile([P, (j1 - j0) * C], BF16, name="x%d" % li)
+            xt_sb = xpool.tile(
+                [P, (j1 - j0) * C], BF16, name="x%d" % li, align_bytes=DMA_ALIGN
+            )
             nc.scalar.dma_start(
                 out=xt_sb[:].rearrange("p (j c) -> p j c", c=C), in_=x_rows[:, j0:j1, :]
             )
@@ -102,7 +105,9 @@ def tile_literatiquantlinear_t_kernel(tc, x, weight, scales, out):
         def multiply(g):
             chunk = (GROUP * g) // STORE
             if chunk not in out_tiles:
-                o_new = opool.tile([P, STORE, O], F32, name="o_sb", tag="o_sb")
+                o_new = opool.tile(
+                    [P, STORE, O], F32, name="o_sb", tag="o_sb", align_bytes=DMA_ALIGN
+                )
                 out_tiles[chunk] = o_new
             o_sb = out_tiles[chunk]
             for jj in range(GROUP):

@@ -18,12 +18,12 @@ ROW_TILES = ROWS // P
 GROUP = 4
 GROUPS = ROW_TILES // GROUP
 DMA_ALIGN = 512
-STORE = 4
 SCALE_MIN = 1e-8
 
 FLOPS = 2 * ROWS * C * O
 
-LOADS = [(0, 4), (4, 8), (8, 16), (16, 32), (32, 48), (48, 64)]
+LOADS = [(0, 4), (4, 16), (16, 36), (36, 64)]
+STORES = [(0, 4), (4, 8)] + [(j, j + 8) for j in range(8, 56, 8)] + [(56, 60), (60, 64)]
 
 
 def tile_literatiquantlinear_t_kernel(tc, x, weight, scales, out):
@@ -36,7 +36,7 @@ def tile_literatiquantlinear_t_kernel(tc, x, weight, scales, out):
         xpool = ctx.enter_context(tc.tile_pool(name="xpool", bufs=1))
         gpool = ctx.enter_context(tc.tile_pool(name="gpool", bufs=3))
         cpool = ctx.enter_context(tc.tile_pool(name="cpool", bufs=3))
-        opool = ctx.enter_context(tc.tile_pool(name="opool", bufs=12))
+        opool = ctx.enter_context(tc.tile_pool(name="opool", bufs=1))
         tpsum = ctx.enter_context(tc.psum_pool(name="tpsum", bufs=4))
         apsum = ctx.enter_context(tc.psum_pool(name="apsum", bufs=4))
         ctx.enter_context(tc.manual_schedule())
@@ -101,17 +101,17 @@ def tile_literatiquantlinear_t_kernel(tc, x, weight, scales, out):
             nc.vector.quantize_mx(out=cd[:].bitcast(FP8X4), scales=pl[:], in_=grouped[g][:])
 
         out_tiles = {}
+        for si, (j0, j1) in enumerate(STORES):
+            o_new = opool.tile(
+                [P, j1 - j0, O], F32, name="o%d" % si, align_bytes=DMA_ALIGN
+            )
+            for j in range(j0, j1):
+                out_tiles[j] = (o_new, j - j0)
+        store_of_last = {j1: (j0, j1) for j0, j1 in STORES}
 
         def multiply(g):
-            chunk = (GROUP * g) // STORE
-            if chunk not in out_tiles:
-                o_new = opool.tile(
-                    [P, STORE, O], F32, name="o_sb", tag="o_sb", align_bytes=DMA_ALIGN
-                )
-                out_tiles[chunk] = o_new
-            o_sb = out_tiles[chunk]
             for jj in range(GROUP):
-                j = GROUP * g + jj
+                o_sb, off = out_tiles[GROUP * g + jj]
                 acc = apsum.tile([P, O], F32, name="acc", tag="acc")
                 nc.tensor.matmul_mx(
                     out=acc[:],
@@ -123,19 +123,13 @@ def tile_literatiquantlinear_t_kernel(tc, x, weight, scales, out):
                     stop=True,
                 )
                 if g % 2 == 1 and jj == 0:
-                    nc.vector.tensor_copy(out=o_sb[:, j % STORE, :], in_=acc[:])
+                    nc.vector.tensor_copy(out=o_sb[:, off, :], in_=acc[:])
                 else:
-                    nc.scalar.copy(out=o_sb[:, j % STORE, :], in_=acc[:])
-            last = chunk == ROW_TILES // STORE - 1
+                    nc.scalar.copy(out=o_sb[:, off, :], in_=acc[:])
             j_end = GROUP * (g + 1)
-            if last:
-                j_start = GROUP * g
-                nc.sync.dma_start(
-                    out=out_rows[:, j_start:j_end, :],
-                    in_=o_sb[:, j_start % STORE : j_start % STORE + GROUP, :],
-                )
-            elif j_end % STORE == 0:
-                nc.sync.dma_start(out=out_rows[:, j_end - STORE : j_end, :], in_=o_sb[:])
+            if j_end in store_of_last:
+                j0, j1 = store_of_last[j_end]
+                nc.sync.dma_start(out=out_rows[:, j0:j1, :], in_=out_tiles[j0][0][:])
 
         s2 = const.tile([P, 16], F32, name="s2")
         nc.vector.tensor_scalar(

from contextlib import ExitStack

import concourse.mybir as mybir
from concourse.masks import make_identity

FP8X4 = mybir.dt.float8_e4m3fn_x4
BF16 = mybir.dt.bfloat16
F32 = mybir.dt.float32
U32 = mybir.dt.uint32
U8 = mybir.dt.uint8
ALU = mybir.AluOpType

P = 128
ROWS = 4 * 2048
C = 512
O = 512
ROW_TILES = ROWS // P
GROUP = 4
GROUPS = ROW_TILES // GROUP
DMA_ALIGN = 512
SCALE_MIN = 1e-8

FLOPS = 2 * ROWS * C * O

LOADS = [(0, 4), (4, 16), (16, 36), (36, 64)]
STORES = [(0, 4), (4, 8)] + [(j, j + 8) for j in range(8, 56, 8)] + [(56, 60), (60, 64)]


def tile_literatiquantlinear_t_kernel(tc, x, weight, scales, out):
    nc = tc.nc
    x_rows = x.rearrange("b (q j) c -> (b q) j c", j=ROW_TILES)
    out_rows = out.rearrange("b (q j) o -> (b q) j o", j=ROW_TILES)

    with ExitStack() as ctx:
        const = ctx.enter_context(tc.tile_pool(name="const", bufs=1))
        xpool = ctx.enter_context(tc.tile_pool(name="xpool", bufs=1))
        gpool = ctx.enter_context(tc.tile_pool(name="gpool", bufs=3))
        cpool = ctx.enter_context(tc.tile_pool(name="cpool", bufs=3))
        opool = ctx.enter_context(tc.tile_pool(name="opool", bufs=1))
        tpsum = ctx.enter_context(tc.psum_pool(name="tpsum", bufs=4))
        apsum = ctx.enter_context(tc.psum_pool(name="apsum", bufs=4))
        ctx.enter_context(tc.manual_schedule())

        s_sb = const.tile([P, 16], BF16, name="s_sb", align_bytes=DMA_ALIGN)
        nc.sync.dma_start(out=s_sb[:], in_=scales.rearrange("(p t) g -> p (t g)", t=4))
        w_sb = const.tile([P, 4, C], BF16, name="w_sb", align_bytes=DMA_ALIGN)
        nc.sync.dma_start(out=w_sb[:], in_=weight.rearrange("(p t) c -> p t c", t=4))
        x_tiles = []
        where = {}
        for li, (j0, j1) in enumerate(LOADS):
            xt_sb = xpool.tile(
                [P, (j1 - j0) * C], BF16, name="x%d" % li, align_bytes=DMA_ALIGN
            )
            nc.scalar.dma_start(
                out=xt_sb[:].rearrange("p (j c) -> p j c", c=C), in_=x_rows[:, j0:j1, :]
            )
            x_tiles.append(xt_sb)
            for j in range(j0, j1):
                where[j] = (li, j - j0)

        ident_f = const.tile([P, P], F32, name="ident_f")
        make_identity(nc, ident_f[:])

        def x_words(j):
            li, off = where[j]
            words = x_tiles[li][:, off * C : (off + 1) * C].bitcast(F32)
            return words.rearrange("p (w u) -> p u w", u=2)

        grouped = {}
        codes = {}
        planes = {}

        def transpose_half(g, h, copy_engine):
            if g not in grouped:
                gr_new = gpool.tile([P, GROUP * C], BF16, name="gr", align_bytes=64)
                grouped[g] = gr_new
            gr_words = grouped[g][:].bitcast(F32)
            xt = tpsum.tile([P, 2, 2, P], F32, name="xt", tag="xt")
            for jj in range(2):
                src = x_words(GROUP * g + 2 * h + jj)
                for u in range(2):
                    nc.tensor.transpose(
                        out=xt[:, jj, u, :], in_=src[:, u, :], identity=ident_f[:]
                    )
            dst = gr_words[:, h * C : (h + 1) * C].rearrange("p (j r u) -> p j r u", j=2, u=2)
            view = xt[:].rearrange("p j u r -> p j r u")
            if copy_engine == "scalar":
                nc.scalar.copy(out=dst, in_=view)
            else:
                nc.vector.tensor_copy(out=dst, in_=view)

        def transposes(g):
            for h in range(GROUP // 2):
                transpose_half(g, h, "vector")

        def quantise(g):
            cd = cpool.tile([P, GROUP * P], U32, name="cd", align_bytes=64)
            pl = cpool.tile([P, GROUP * P], U8, name="pl", align_bytes=64)
            codes[g] = cd
            planes[g] = pl
            nc.vector.quantize_mx(out=cd[:].bitcast(FP8X4), scales=pl[:], in_=grouped[g][:])

        out_tiles = {}
        for si, (j0, j1) in enumerate(STORES):
            o_new = opool.tile(
                [P, j1 - j0, O], F32, name="o%d" % si, align_bytes=DMA_ALIGN
            )
            for j in range(j0, j1):
                out_tiles[j] = (o_new, j - j0)
        store_of_last = {j1: (j0, j1) for j0, j1 in STORES}

        def multiply(g):
            for jj in range(GROUP):
                o_sb, off = out_tiles[GROUP * g + jj]
                acc = apsum.tile([P, O], F32, name="acc", tag="acc")
                nc.tensor.matmul_mx(
                    out=acc[:],
                    lhsT=codes[g][:, jj * P : (jj + 1) * P].bitcast(FP8X4),
                    lhsT_scale=planes[g][:, jj * P : (jj + 1) * P],
                    rhs=w_codes[:].bitcast(FP8X4),
                    rhs_scale=w_plane[:],
                    start=True,
                    stop=True,
                )
                if g % 2 == 1 and jj == 0:
                    nc.vector.tensor_copy(out=o_sb[:, off, :], in_=acc[:])
                else:
                    nc.scalar.copy(out=o_sb[:, off, :], in_=acc[:])
            j_end = GROUP * (g + 1)
            if j_end in store_of_last:
                j0, j1 = store_of_last[j_end]
                nc.sync.dma_start(out=out_rows[:, j0:j1, :], in_=out_tiles[j0][0][:])

        s2 = const.tile([P, 16], F32, name="s2")
        nc.vector.tensor_scalar(
            out=s2[:],
            in0=s_sb[:],
            scalar1=SCALE_MIN,
            scalar2=2.0,
            op0=ALU.max,
            op1=ALU.mult,
        )
        half = const.tile([P, 4, C], BF16, name="half")
        wq = const.tile([P, 4, C], BF16, name="wq")
        wg = const.tile([P, O * 4], BF16, name="wg", align_bytes=64)
        wg_words = wg[:].bitcast(F32).rearrange("p (r ot u) -> p r ot u", ot=4, u=2)

        def signs_times_scales(h):
            nc.vector.tensor_scalar(
                out=half[:, 2 * h : 2 * h + 2, :],
                in0=w_sb[:, 2 * h : 2 * h + 2, :],
                scalar1=0.0,
                scalar2=0.5,
                op0=ALU.is_ge,
                op1=ALU.subtract,
            )
            for ot in (2 * h, 2 * h + 1):
                for g in range(4):
                    cols = slice(g * P, (g + 1) * P)
                    nc.vector.tensor_scalar(
                        out=wq[:, ot, cols],
                        in0=half[:, ot, cols],
                        scalar1=s2[:, 4 * ot + g : 4 * ot + g + 1],
                        scalar2=None,
                        op0=ALU.mult,
                    )

        def weight_transposes(h):
            wt = tpsum.tile([P, 2, 2, P], F32, name="wt", tag="xt")
            for oo in range(2):
                words = wq[:, 2 * h + oo, :].bitcast(F32).rearrange("p (w u) -> p u w", u=2)
                for u in range(2):
                    nc.tensor.transpose(
                        out=wt[:, oo, u, :], in_=words[:, u, :], identity=ident_f[:]
                    )
            nc.scalar.copy(
                out=wg_words[:, :, 2 * h : 2 * h + 2, :],
                in_=wt[:].rearrange("p ot u r -> p r ot u"),
            )

        signs_times_scales(0)
        signs_times_scales(1)
        weight_transposes(0)
        transpose_half(0, 0, "vector")
        weight_transposes(1)
        transpose_half(0, 1, "scalar")
        w_codes = const.tile([P, O], U32, name="w_codes", align_bytes=64)
        w_plane = const.tile([P, O], U8, name="w_plane", align_bytes=64)
        nc.vector.quantize_mx(
            out=w_codes[:].bitcast(FP8X4),
            scales=w_plane[:],
            in_=wg[:],
        )
        quantise(0)

        for i in range(1, GROUPS + 2):
            if i < GROUPS:
                transposes(i)
            if 2 <= i <= GROUPS:
                quantise(i - 1)
            if i >= 2:
                multiply(i - 2)
